import numpy as np
import ml_dtypes


def mxq(x, axis, fmt="e4m3"):
    dtype, down = {"e4m3": (ml_dtypes.float8_e4m3fn, 7), "e5m2": (ml_dtypes.float8_e5m2, 14)}[fmt]
    v = np.moveaxis(np.asarray(x, np.float32).astype(ml_dtypes.bfloat16).astype(np.float64), axis, -1)
    blocks = v.reshape(v.shape[:-1] + (-1, 32))
    amax = np.abs(blocks).max(-1, keepdims=True)
    byte = np.maximum(np.where(amax > 0, np.frexp(amax)[1] - 1 + 127, 0) - down, 1)
    scale = np.exp2(byte - 127.0)
    codes = (blocks / scale).astype(np.float32).astype(dtype).astype(np.float64)
    return np.moveaxis((codes * scale).reshape(v.shape), -1, axis)


WIDE = False


def mx_kscale(k):
    if not WIDE:
        return np.ones(k)
    levels = np.array([10, -10, 5, -5, 0])
    a = np.random.permutation(np.resize(levels, k // 512 * 4)).reshape(k // 512, 4)
    idx = np.arange(k)
    return np.exp2(a[idx // 512, idx % 128 // 32])


BF16 = ml_dtypes.bfloat16


def bf(x):
    return np.asarray(x, np.float32).astype(BF16)


def f64(x):
    return np.asarray(x).astype(np.float64)


B, S, H, NH, D, C = 8, 512, 512, 3, 128, 512
V = S


def setup_inputs():
    s = mx_kscale(H)
    return {
        "qh": bf(np.random.standard_normal((NH, B, S, D)) * 1.4),
        "kh": bf(np.random.standard_normal((NH, B, S, D)) * 1.4),
        "v": bf(np.random.standard_normal((B, S, H)) * s),
        "Wv": bf(np.random.standard_normal((H, V)) * 2.0 / np.sqrt(H) / s[:, None]),
        "bv": bf(np.random.standard_normal(V) * 0.3),
    }


def reference(qh, kh, v, Wv, bv):
    qh, kh = f64(qh), f64(kh)
    vv = (mxq(f64(v), 2, "e4m3") @ mxq(f64(Wv), 0, "e4m3")) + f64(bv)
    vq = mxq(vv, 1, "e4m3")
    mask = np.triu(np.full((S, S), -np.inf), 1)
    out = np.zeros((B, S, V))
    for r in range(0, S, C):
        t = r + C
        sc = qh[:, :, r:t] @ kh[:, :, :t].transpose(0, 1, 3, 2) * D ** (-0.5) + mask[r:t, :t]
        e = np.exp(sc - sc.max(-1, keepdims=True))
        p = e / e.sum(-1, keepdims=True)
        out[:, r:t] = (mxq(p, 3, "e4m3") @ vq[:, :t]).mean(0)
    return out

@@ -1,0 +1,243 @@
+from contextlib import ExitStack
+
+import concourse.mybir as mybir
+from concourse.masks import make_identity
+
+F32 = mybir.dt.float32
+BF16 = mybir.dt.bfloat16
+U32 = mybir.dt.uint32
+U8 = mybir.dt.uint8
+FP8X4 = mybir.dt.float8_e4m3fn_x4
+ALU = mybir.AluOpType
+ACT = mybir.ActivationFunctionType
+
+P = 128
+PACK = 4
+NH, B, S, D = 3, 8, 512, 128
+H = 512
+V = 512
+CHUNKS = S // P
+SCALE = D ** -0.5
+MASKED = -1.0e30
+
+FLOPS = 2 * (B * S * H * V + NH * B * S * S * D + NH * B * S * S * V)
+
+
+def tile_interpretablemultiheadattention_pa_t_kernel(tc, qh, kh, v, Wv, bv, out):
+    nc = tc.nc
+    with ExitStack() as ctx:
+        const = ctx.enter_context(tc.tile_pool(name="const", bufs=1))
+        inputs = ctx.enter_context(tc.tile_pool(name="inputs", bufs=1))
+        work = ctx.enter_context(tc.tile_pool(name="work", bufs=3))
+        blocks = ctx.enter_context(tc.tile_pool(name="blocks", bufs=6))
+        batch = ctx.enter_context(tc.tile_pool(name="batch", bufs=2))
+        heads = ctx.enter_context(tc.tile_pool(name="heads", bufs=2 * NH))
+        stores = ctx.enter_context(tc.tile_pool(name="stores", bufs=4))
+        ps_scores = ctx.enter_context(tc.psum_pool(name="ps_scores", bufs=3))
+        ps_pt = ctx.enter_context(tc.psum_pool(name="ps_pt", bufs=2))
+        ps_qk = ctx.enter_context(tc.psum_pool(name="ps_qk", bufs=1))
+        ps_mx = ctx.enter_context(tc.psum_pool(name="ps_mx", bufs=2))
+
+        w_raw = const.tile([P, PACK, V], BF16)
+        nc.sync.dma_start(
+            out=w_raw[:].rearrange("q (u e) c -> q u e c", u=2),
+            in_=Wv.rearrange("(u q e) c -> q u e c", u=2, e=2),
+        )
+        bias = const.tile([P, V], BF16)
+        nc.sync.dma_start(out=bias[:], in_=bv.partition_broadcast(P))
+        v_sb, q_sb, k_sb = [], [], []
+        for b in range(B):
+            v_b = inputs.tile([P, CHUNKS, H], BF16, name="v%d" % b)
+            nc.sync.dma_start(out=v_b[:], in_=v[b].rearrange("(c p) h -> p c h", p=P))
+            v_sb.append(v_b)
+            for n in range(NH):
+                q_u = inputs.tile([P, CHUNKS, D], BF16, name="q%d_%d" % (b, n))
+                nc.sync.dma_start(out=q_u[:], in_=qh[n, b].rearrange("(c p) d -> p c d", p=P))
+                q_sb.append(q_u)
+                k_u = inputs.tile([P, CHUNKS, D], BF16, name="k%d_%d" % (b, n))
+                nc.sync.dma_start(out=k_u[:], in_=kh[n, b].rearrange("(c p) d -> p c d", p=P))
+                k_sb.append(k_u)
+
+        ident_bf = const.tile([P, P], BF16)
+        make_identity(nc, ident_bf[:])
+        ident_f32 = const.tile([P, P], F32)
+        make_identity(nc, ident_f32[:])
+        mask_f32 = const.tile([P, P], F32)
+        nc.gpsimd.memset(mask_f32[:], 0.0)
+        nc.gpsimd.affine_select(
+            out=mask_f32[:],
+            in_=mask_f32[:],
+            compare_op=ALU.is_ge,
+            fill=MASKED,
+            base=0,
+            pattern=[[-1, P]],
+            channel_multiplier=1,
+        )
+        mask_bf = const.tile([P, P], BF16)
+        nc.vector.tensor_copy(out=mask_bf[:], in_=mask_f32[:])
+
+        p_grouped = []
+        for x in range(3):
+            g = const.tile([P, S, PACK], BF16, name="p_grouped%d" % x, align_bytes=64)
+            nc.vector.memset(g[:], 0.0)
+            p_grouped.append(g)
+
+        w_grouped = const.tile([P, V, PACK], BF16, align_bytes=64)
+        nc.vector.tensor_copy(out=w_grouped[:], in_=w_raw[:].rearrange("q t c -> q c t"))
+        w_codes = const.tile([P, V], U32, align_bytes=64)
+        w_scales = const.tile([P, V], U8, align_bytes=64)
+        nc.vector.quantize_mx(
+            out=w_codes[:].bitcast(FP8X4),
+            scales=w_scales[:],
+            in_=w_grouped[:].rearrange("q c t -> q (c t)"),
+        )
+
+        for b in range(B):
+            v_words = v_sb[b][:].rearrange("p c h -> p (c h)").bitcast(F32)
+            v_grouped = batch.tile([P, S, PACK], BF16, align_bytes=64)
+            v_grouped_words = v_grouped[:].rearrange("p r t -> p (r t)").bitcast(F32)
+            for half in range(2):
+                vt = ps_mx.tile([P, 2, 2, P], F32, tag="mx")
+                for c in range(2):
+                    for u in range(2):
+                        first = (2 * half + c) * (H // 2) + u * P
+                        nc.tensor.transpose(
+                            vt[:, c, u, :], v_words[:, first : first + P], ident_f32[:]
+                        )
+                nc.scalar.copy(
+                    out=v_grouped_words[:, half * S : (half + 1) * S].rearrange(
+                        "p (c r u) -> p c r u", c=2, u=2
+                    ),
+                    in_=vt[:].rearrange("p c u r -> p c r u"),
+                )
+            v_codes = batch.tile([P, S], U32, align_bytes=64)
+            v_scales = batch.tile([P, S], U8, align_bytes=64)
+            nc.vector.quantize_mx(
+                out=v_codes[:].bitcast(FP8X4),
+                scales=v_scales[:],
+                in_=v_grouped[:].rearrange("p r t -> p (r t)"),
+            )
+            vv_grouped = batch.tile([P, V, PACK], BF16, align_bytes=64)
+            for w in range(V // P):
+                cols = slice(w * P, (w + 1) * P)
+                vv_ps = ps_mx.tile([P, PACK, P], F32, tag="mx")
+                for t in range(PACK):
+                    toks = slice(t * P, (t + 1) * P)
+                    nc.tensor.matmul_mx(
+                        out=vv_ps[:, t, :],
+                        lhsT=v_codes[:, toks].bitcast(FP8X4),
+                        lhsT_scale=v_scales[:, toks],
+                        rhs=w_codes[:, cols].bitcast(FP8X4),
+                        rhs_scale=w_scales[:, cols],
+                        start=True,
+                        stop=True,
+                    )
+                nc.vector.tensor_tensor(
+                    out=vv_grouped[:, cols, :],
+                    in0=vv_ps[:].rearrange("p t c -> p c t"),
+                    in1=bias[:, cols].unsqueeze(2).to_broadcast([P, P, PACK]),
+                    op=ALU.add,
+                )
+            vv_codes = batch.tile([P, V], U32, align_bytes=64)
+            vv_scales = batch.tile([P, V], U8, align_bytes=64)
+            nc.vector.quantize_mx(
+                out=vv_codes[:].bitcast(FP8X4),
+                scales=vv_scales[:],
+                in_=vv_grouped[:].rearrange("p c t -> p (c t)"),
+            )
+
+            p_codes, p_scales = [], []
+            for n in range(NH):
+                unit = b * NH + n
+                qk_ps = ps_qk.tile([P, 2, S], BF16)
+                for c in range(CHUNKS):
+                    nc.tensor.transpose(qk_ps[:, 0, c * P : (c + 1) * P], q_sb[unit][:, c, :], ident_bf[:])
+                for c in range(CHUNKS):
+                    nc.tensor.transpose(qk_ps[:, 1, c * P : (c + 1) * P], k_sb[unit][:, c, :], ident_bf[:])
+                qk_t = work.tile([P, 2, S], BF16)
+                nc.scalar.copy(out=qk_t[:], in_=qk_ps[:])
+
+                grouped = p_grouped[unit % 3]
+                neg_max = work.tile([P, CHUNKS], F32)
+                row_sum = work.tile([P, CHUNKS], F32)
+                inv_sum = work.tile([P, CHUNKS], F32)
+                for i in range(CHUNKS):
+                    keys = (i + 1) * P
+                    rows = slice(i * P, (i + 1) * P)
+                    sc = ps_scores.tile([P, S], F32)
+                    nc.tensor.matmul(
+                        out=sc[:, 0:keys],
+                        lhsT=qk_t[:, 0, rows],
+                        rhs=qk_t[:, 1, 0:keys],
+                        start=True,
+                        stop=False,
+                    )
+                    nc.tensor.matmul(
+                        out=sc[:, rows], lhsT=ident_bf[:], rhs=mask_bf[:], start=False, stop=True
+                    )
+                    e = blocks.tile([P, S], F32)
+                    nc.vector.tensor_scalar(
+                        out=e[:, 0:keys],
+                        in0=sc[:, 0:keys],
+                        scalar1=-SCALE,
+                        scalar2=None,
+                        op0=ALU.mult,
+                        op1=ALU.min,
+                        accum_out=neg_max[:, i : i + 1],
+                    )
+                    nc.scalar.activation(
+                        out=e[:, 0:keys],
+                        in_=e[:, 0:keys],
+                        func=ACT.Exp,
+                        bias=neg_max[:, i : i + 1],
+                        scale=-1.0,
+                        accum_out=row_sum[:, i : i + 1],
+                    )
+                    nc.vector.reciprocal(out=inv_sum[:, i : i + 1], in_=row_sum[:, i : i + 1])
+                    p_bf = blocks.tile([P, S], BF16)
+                    nc.vector.tensor_scalar(
+                        out=p_bf[:, 0:keys],
+                        in0=e[:, 0:keys],
+                        scalar1=inv_sum[:, i : i + 1],
+                        scalar2=None,
+                        op0=ALU.mult,
+                    )
+                    pt = ps_pt.tile([P, PACK, P], BF16)
+                    for t in range(i + 1):
+                        nc.tensor.transpose(pt[:, t, :], p_bf[:, t * P : (t + 1) * P], ident_bf[:])
+                    if i == CHUNKS - 1:
+                        nc.vector.tensor_copy(
+                            out=grouped[:, rows, 0 : i + 1],
+                            in_=pt[:, 0 : i + 1, :].rearrange("p t q -> p q t"),
+                        )
+                    else:
+                        nc.scalar.copy(
+                            out=grouped[:, rows, 0 : i + 1],
+                            in_=pt[:, 0 : i + 1, :].rearrange("p t q -> p q t"),
+                        )
+                codes = heads.tile([P, S], U32, align_bytes=64)
+                scales = heads.tile([P, S], U8, align_bytes=64)
+                nc.vector.quantize_mx(
+                    out=codes[:].bitcast(FP8X4),
+                    scales=scales[:],
+                    in_=grouped[:].rearrange("p q t -> p (q t)"),
+                )
+                p_codes.append(codes)
+                p_scales.append(scales)
+
+            for i in range(CHUNKS):
+                rows = slice(i * P, (i + 1) * P)
+                acc = ps_mx.tile([P, V], F32, tag="mx")
+                for n in range(NH):
+                    nc.tensor.matmul_mx(
+                        out=acc[:],
+                        lhsT=p_codes[n][:, rows].bitcast(FP8X4),
+                        lhsT_scale=p_scales[n][:, rows],
+                        rhs=vv_codes[:].bitcast(FP8X4),
+                        rhs_scale=vv_scales[:],
+                        start=(n == 0),
+                        stop=(n == NH - 1),
+                    )
+                result = stores.tile([P, V], F32)
+                nc.scalar.mul(out=result[:], in_=acc[:], mul=1.0 / NH)
+                nc.sync.dma_start(out=out[b, rows, :], in_=result[:])

@@ -17,6 +17,9 @@ NH, B, S, D = 3, 8, 512, 128
 H = 512
 V = 512
 CHUNKS = S // P
+UNITS = B * NH
+FIRST = [P * i * (i + 1) // 2 for i in range(CHUNKS)]
+WIDTH = P * CHUNKS * (CHUNKS + 1) // 2
 SCALE = D ** -0.5
 MASKED = -1.0e30
 
@@ -28,28 +31,16 @@ def tile_interpretablemultiheadattention_pa_t_kernel(tc, qh, kh, v, Wv, bv, out)
     with ExitStack() as ctx:
         const = ctx.enter_context(tc.tile_pool(name="const", bufs=1))
         inputs = ctx.enter_context(tc.tile_pool(name="inputs", bufs=1))
-        work = ctx.enter_context(tc.tile_pool(name="work", bufs=3))
-        blocks = ctx.enter_context(tc.tile_pool(name="blocks", bufs=6))
-        batch = ctx.enter_context(tc.tile_pool(name="batch", bufs=2))
-        heads = ctx.enter_context(tc.tile_pool(name="heads", bufs=2 * NH))
+        per_unit = ctx.enter_context(tc.tile_pool(name="per_unit", bufs=3))
+        per_batch = ctx.enter_context(tc.tile_pool(name="per_batch", bufs=2))
         stores = ctx.enter_context(tc.tile_pool(name="stores", bufs=4))
-        ps_scores = ctx.enter_context(tc.psum_pool(name="ps_scores", bufs=3))
-        ps_pt = ctx.enter_context(tc.psum_pool(name="ps_pt", bufs=2))
-        ps_qk = ctx.enter_context(tc.psum_pool(name="ps_qk", bufs=1))
-        ps_mx = ctx.enter_context(tc.psum_pool(name="ps_mx", bufs=2))
+        psum = ctx.enter_context(tc.psum_pool(name="psum", bufs=8))
+        ctx.enter_context(tc.manual_schedule())
 
-        w_raw = const.tile([P, PACK, V], BF16)
-        nc.sync.dma_start(
-            out=w_raw[:].rearrange("q (u e) c -> q u e c", u=2),
-            in_=Wv.rearrange("(u q e) c -> q u e c", u=2, e=2),
-        )
-        bias = const.tile([P, V], BF16)
-        nc.sync.dma_start(out=bias[:], in_=bv.partition_broadcast(P))
         v_sb, q_sb, k_sb = [], [], []
+        w_raw = const.tile([P, PACK, V], BF16)
+        bias = const.tile([P, V], BF16)
         for b in range(B):
-            v_b = inputs.tile([P, CHUNKS, H], BF16, name="v%d" % b)
-            nc.sync.dma_start(out=v_b[:], in_=v[b].rearrange("(c p) h -> p c h", p=P))
-            v_sb.append(v_b)
             for n in range(NH):
                 q_u = inputs.tile([P, CHUNKS, D], BF16, name="q%d_%d" % (b, n))
                 nc.sync.dma_start(out=q_u[:], in_=qh[n, b].rearrange("(c p) d -> p c d", p=P))
@@ -57,11 +48,18 @@ def tile_interpretablemultiheadattention_pa_t_kernel(tc, qh, kh, v, Wv, bv, out)
                 k_u = inputs.tile([P, CHUNKS, D], BF16, name="k%d_%d" % (b, n))
                 nc.sync.dma_start(out=k_u[:], in_=kh[n, b].rearrange("(c p) d -> p c d", p=P))
                 k_sb.append(k_u)
+            v_b = inputs.tile([P, CHUNKS, H], BF16, name="v%d" % b)
+            nc.sync.dma_start(out=v_b[:], in_=v[b].rearrange("(c p) h -> p c h", p=P))
+            v_sb.append(v_b)
+            if b == 0:
+                nc.sync.dma_start(
+                    out=w_raw[:].rearrange("q (u e) c -> q u e c", u=2),
+                    in_=Wv.rearrange("(u q e) c -> q u e c", u=2, e=2),
+                )
+                nc.sync.dma_start(out=bias[:], in_=bv.partition_broadcast(P))
 
         ident_bf = const.tile([P, P], BF16)
         make_identity(nc, ident_bf[:])
-        ident_f32 = const.tile([P, P], F32)
-        make_identity(nc, ident_f32[:])
         mask_f32 = const.tile([P, P], F32)
         nc.gpsimd.memset(mask_f32[:], 0.0)
         nc.gpsimd.affine_select(
@@ -75,169 +73,290 @@ def tile_interpretablemultiheadattention_pa_t_kernel(tc, qh, kh, v, Wv, bv, out)
         )
         mask_bf = const.tile([P, P], BF16)
         nc.vector.tensor_copy(out=mask_bf[:], in_=mask_f32[:])
-
+        ident_f32 = const.tile([P, P], F32)
+        make_identity(nc, ident_f32[:])
         p_grouped = []
         for x in range(3):
             g = const.tile([P, S, PACK], BF16, name="p_grouped%d" % x, align_bytes=64)
-            nc.vector.memset(g[:], 0.0)
+            nc.gpsimd.memset(g[:], 0.0)
             p_grouped.append(g)
-
         w_grouped = const.tile([P, V, PACK], BF16, align_bytes=64)
-        nc.vector.tensor_copy(out=w_grouped[:], in_=w_raw[:].rearrange("q t c -> q c t"))
         w_codes = const.tile([P, V], U32, align_bytes=64)
         w_scales = const.tile([P, V], U8, align_bytes=64)
-        nc.vector.quantize_mx(
-            out=w_codes[:].bitcast(FP8X4),
-            scales=w_scales[:],
-            in_=w_grouped[:].rearrange("q c t -> q (c t)"),
-        )
 
-        for b in range(B):
+        live = {}
+
+        def transpose_v(b):
             v_words = v_sb[b][:].rearrange("p c h -> p (c h)").bitcast(F32)
-            v_grouped = batch.tile([P, S, PACK], BF16, align_bytes=64)
-            v_grouped_words = v_grouped[:].rearrange("p r t -> p (r t)").bitcast(F32)
             for half in range(2):
-                vt = ps_mx.tile([P, 2, 2, P], F32, tag="mx")
+                vt = psum.tile([P, 2, 2, P], F32, name="vt", tag="bank")
                 for c in range(2):
                     for u in range(2):
                         first = (2 * half + c) * (H // 2) + u * P
                         nc.tensor.transpose(
                             vt[:, c, u, :], v_words[:, first : first + P], ident_f32[:]
                         )
+                live["vt", b, half] = vt
+
+        def group_v(b):
+            v_grouped = per_batch.tile([P, S, PACK], BF16, name="v_grouped", align_bytes=64)
+            words = v_grouped[:].rearrange("p r t -> p (r t)").bitcast(F32)
+            for half in range(2):
                 nc.scalar.copy(
-                    out=v_grouped_words[:, half * S : (half + 1) * S].rearrange(
+                    out=words[:, half * S : (half + 1) * S].rearrange(
                         "p (c r u) -> p c r u", c=2, u=2
                     ),
-                    in_=vt[:].rearrange("p c u r -> p c r u"),
+                    in_=live["vt", b, half][:].rearrange("p c u r -> p c r u"),
                 )
-            v_codes = batch.tile([P, S], U32, align_bytes=64)
-            v_scales = batch.tile([P, S], U8, align_bytes=64)
+            live["v_grouped", b] = v_grouped
+            if b == 0:
+                nc.vector.tensor_copy(out=w_grouped[:], in_=w_raw[:].rearrange("q t c -> q c t"))
+
+        def quantise_v(b):
+            v_codes = per_batch.tile([P, S], U32, name="v_codes", align_bytes=64)
+            v_scales = per_batch.tile([P, S], U8, name="v_scales", align_bytes=64)
             nc.vector.quantize_mx(
                 out=v_codes[:].bitcast(FP8X4),
                 scales=v_scales[:],
-                in_=v_grouped[:].rearrange("p r t -> p (r t)"),
+                in_=live["v_grouped", b][:].rearrange("p r t -> p (r t)"),
             )
-            vv_grouped = batch.tile([P, V, PACK], BF16, align_bytes=64)
-            for w in range(V // P):
+            live["v_codes", b] = v_codes
+            live["v_scales", b] = v_scales
+            if b == 0:
+                nc.vector.quantize_mx(
+                    out=w_codes[:].bitcast(FP8X4),
+                    scales=w_scales[:],
+                    in_=w_grouped[:].rearrange("q c t -> q (c t)"),
+                )
+
+        def multiply_vv(b, pieces):
+            for w in pieces:
                 cols = slice(w * P, (w + 1) * P)
-                vv_ps = ps_mx.tile([P, PACK, P], F32, tag="mx")
+                vv_ps = psum.tile([P, PACK, P], F32, name="vv_ps", tag="bank")
                 for t in range(PACK):
                     toks = slice(t * P, (t + 1) * P)
                     nc.tensor.matmul_mx(
                         out=vv_ps[:, t, :],
-                        lhsT=v_codes[:, toks].bitcast(FP8X4),
-                        lhsT_scale=v_scales[:, toks],
+                        lhsT=live["v_codes", b][:, toks].bitcast(FP8X4),
+                        lhsT_scale=live["v_scales", b][:, toks],
                         rhs=w_codes[:, cols].bitcast(FP8X4),
                         rhs_scale=w_scales[:, cols],
                         start=True,
                         stop=True,
                     )
+                live["vv_ps", b, w] = vv_ps
+
+        def add_bias(b, pieces):
+            if 0 in pieces:
+                live["vv_grouped", b] = per_batch.tile(
+                    [P, V, PACK], BF16, name="vv_grouped", align_bytes=64
+                )
+            for w in pieces:
+                cols = slice(w * P, (w + 1) * P)
                 nc.vector.tensor_tensor(
-                    out=vv_grouped[:, cols, :],
-                    in0=vv_ps[:].rearrange("p t c -> p c t"),
+                    out=live["vv_grouped", b][:, cols, :],
+                    in0=live["vv_ps", b, w][:].rearrange("p t c -> p c t"),
                     in1=bias[:, cols].unsqueeze(2).to_broadcast([P, P, PACK]),
                     op=ALU.add,
                 )
-            vv_codes = batch.tile([P, V], U32, align_bytes=64)
-            vv_scales = batch.tile([P, V], U8, align_bytes=64)
+
+        def quantise_vv(b):
+            vv_codes = per_batch.tile([P, V], U32, name="vv_codes", align_bytes=64)
+            vv_scales = per_batch.tile([P, V], U8, name="vv_scales", align_bytes=64)
             nc.vector.quantize_mx(
                 out=vv_codes[:].bitcast(FP8X4),
                 scales=vv_scales[:],
-                in_=vv_grouped[:].rearrange("p c t -> p (c t)"),
+                in_=live["vv_grouped", b][:].rearrange("p c t -> p (c t)"),
             )
+            live["vv_codes", b] = vv_codes
+            live["vv_scales", b] = vv_scales
 
-            p_codes, p_scales = [], []
-            for n in range(NH):
-                unit = b * NH + n
-                qk_ps = ps_qk.tile([P, 2, S], BF16)
-                for c in range(CHUNKS):
-                    nc.tensor.transpose(qk_ps[:, 0, c * P : (c + 1) * P], q_sb[unit][:, c, :], ident_bf[:])
-                for c in range(CHUNKS):
-                    nc.tensor.transpose(qk_ps[:, 1, c * P : (c + 1) * P], k_sb[unit][:, c, :], ident_bf[:])
-                qk_t = work.tile([P, 2, S], BF16)
-                nc.scalar.copy(out=qk_t[:], in_=qk_ps[:])
+        def transpose_qk(unit):
+            qk_ps = psum.tile([P, 2, S], BF16, name="qk_ps", tag="bank")
+            for c in range(CHUNKS):
+                nc.tensor.transpose(qk_ps[:, 0, c * P : (c + 1) * P], q_sb[unit][:, c, :], ident_bf[:])
+            for c in range(CHUNKS):
+                nc.tensor.transpose(qk_ps[:, 1, c * P : (c + 1) * P], k_sb[unit][:, c, :], ident_bf[:])
+            live["qk_ps", unit] = qk_ps
 
-                grouped = p_grouped[unit % 3]
-                neg_max = work.tile([P, CHUNKS], F32)
-                row_sum = work.tile([P, CHUNKS], F32)
-                inv_sum = work.tile([P, CHUNKS], F32)
-                for i in range(CHUNKS):
+        def copy_qk(unit):
+            qk_t = per_unit.tile([P, 2, S], BF16, name="qk_t")
+            nc.scalar.copy(out=qk_t[:], in_=live["qk_ps", unit][:])
+            live["qk_t", unit] = qk_t
+
+        SCORE_BANKS = [[3], [2, 0], [1]]
+
+        def scores(unit):
+            qk_t = live["qk_t", unit]
+            for blocks in SCORE_BANKS:
+                sc = psum.tile([P, S], F32, name="sc", tag="bank")
+                first = 0
+                for i in blocks:
                     keys = (i + 1) * P
                     rows = slice(i * P, (i + 1) * P)
-                    sc = ps_scores.tile([P, S], F32)
                     nc.tensor.matmul(
-                        out=sc[:, 0:keys],
+                        out=sc[:, first : first + keys],
                         lhsT=qk_t[:, 0, rows],
                         rhs=qk_t[:, 1, 0:keys],
                         start=True,
                         stop=False,
                     )
                     nc.tensor.matmul(
-                        out=sc[:, rows], lhsT=ident_bf[:], rhs=mask_bf[:], start=False, stop=True
+                        out=sc[:, first + i * P : first + keys],
+                        lhsT=ident_bf[:],
+                        rhs=mask_bf[:],
+                        start=False,
+                        stop=True,
                     )
-                    e = blocks.tile([P, S], F32)
+                    live["sc", unit, i] = sc[:, first : first + keys]
+                    first += keys
+
+        def row_max(unit):
+            neg_max = per_unit.tile([P, CHUNKS], F32, name="neg_max")
+            e = per_unit.tile([P, WIDTH], F32, name="e")
+            for blocks in SCORE_BANKS:
+                for i in blocks:
                     nc.vector.tensor_scalar(
-                        out=e[:, 0:keys],
-                        in0=sc[:, 0:keys],
+                        out=e[:, FIRST[i] : FIRST[i] + (i + 1) * P],
+                        in0=live["sc", unit, i],
                         scalar1=-SCALE,
                         scalar2=None,
                         op0=ALU.mult,
                         op1=ALU.min,
                         accum_out=neg_max[:, i : i + 1],
                     )
+            live["neg_max", unit] = neg_max
+            live["e", unit] = e
+
+        def exponential(unit):
+            row_sum = per_unit.tile([P, CHUNKS], F32, name="row_sum")
+            e = live["e", unit]
+            for blocks in SCORE_BANKS:
+                for i in blocks:
+                    cols = slice(FIRST[i], FIRST[i] + (i + 1) * P)
                     nc.scalar.activation(
-                        out=e[:, 0:keys],
-                        in_=e[:, 0:keys],
+                        out=e[:, cols],
+                        in_=e[:, cols],
                         func=ACT.Exp,
-                        bias=neg_max[:, i : i + 1],
+                        bias=live["neg_max", unit][:, i : i + 1],
                         scale=-1.0,
                         accum_out=row_sum[:, i : i + 1],
                     )
-                    nc.vector.reciprocal(out=inv_sum[:, i : i + 1], in_=row_sum[:, i : i + 1])
-                    p_bf = blocks.tile([P, S], BF16)
-                    nc.vector.tensor_scalar(
-                        out=p_bf[:, 0:keys],
-                        in0=e[:, 0:keys],
-                        scalar1=inv_sum[:, i : i + 1],
-                        scalar2=None,
-                        op0=ALU.mult,
-                    )
-                    pt = ps_pt.tile([P, PACK, P], BF16)
-                    for t in range(i + 1):
-                        nc.tensor.transpose(pt[:, t, :], p_bf[:, t * P : (t + 1) * P], ident_bf[:])
-                    if i == CHUNKS - 1:
-                        nc.vector.tensor_copy(
-                            out=grouped[:, rows, 0 : i + 1],
-                            in_=pt[:, 0 : i + 1, :].rearrange("p t q -> p q t"),
-                        )
-                    else:
-                        nc.scalar.copy(
-                            out=grouped[:, rows, 0 : i + 1],
-                            in_=pt[:, 0 : i + 1, :].rearrange("p t q -> p q t"),
-                        )
-                codes = heads.tile([P, S], U32, align_bytes=64)
-                scales = heads.tile([P, S], U8, align_bytes=64)
-                nc.vector.quantize_mx(
-                    out=codes[:].bitcast(FP8X4),
-                    scales=scales[:],
-                    in_=grouped[:].rearrange("p q t -> p (q t)"),
-                )
-                p_codes.append(codes)
-                p_scales.append(scales)
+            live["row_sum", unit] = row_sum
 
-            for i in range(CHUNKS):
+        def reciprocal(unit):
+            inv_sum = per_unit.tile([P, CHUNKS], F32, name="inv_sum")
+            nc.vector.reciprocal(out=inv_sum[:], in_=live["row_sum", unit][:])
+            live["inv_sum", unit] = inv_sum
+
+        P_BANKS = [[3, 0], [2, 1]]
+
+        def normalise(unit):
+            p_bf = per_unit.tile([P, WIDTH], BF16, name="p_bf")
+            for blocks in P_BANKS:
+                for i in blocks:
+                    cols = slice(FIRST[i], FIRST[i] + (i + 1) * P)
+                    nc.gpsimd.tensor_scalar(
+                        out=p_bf[:, cols],
+                        in0=live["e", unit][:, cols],
+                        scalar1=live["inv_sum", unit][:, i : i + 1],
+                        scalar2=0.0,
+                        op0=ALU.mult,
+                        op1=ALU.add,
+                    )
+            live["p_bf", unit] = p_bf
+
+        def transpose_p(unit):
+            p_bf = live["p_bf", unit]
+            for blocks in P_BANKS:
+                pt = psum.tile([P, CHUNKS + 1, P], BF16, name="pt", tag="bank")
+                plane = 0
+                for i in blocks:
+                    for t in range(i + 1):
+                        nc.tensor.transpose(
+                            pt[:, plane + t, :],
+                            p_bf[:, FIRST[i] + t * P : FIRST[i] + (t + 1) * P],
+                            ident_bf[:],
+                        )
+                    live["pt", unit, i] = pt[:, plane : plane + i + 1, :]
+                    plane += i + 1
+
+        def group_p(unit):
+            for i in P_BANKS[0]:
+                nc.vector.tensor_copy(
+                    out=p_grouped[unit % 3][:, i * P : (i + 1) * P, 0 : i + 1],
+                    in_=live["pt", unit, i].rearrange("p t q -> p q t"),
+                )
+            for i in P_BANKS[1]:
+                nc.scalar.copy(
+                    out=p_grouped[unit % 3][:, i * P : (i + 1) * P, 0 : i + 1],
+                    in_=live["pt", unit, i].rearrange("p t q -> p q t"),
+                )
+
+        def quantise_p(unit):
+            p_codes = per_unit.tile([P, S], U32, name="p_codes", bufs=2 * NH, align_bytes=64)
+            p_scales = per_unit.tile([P, S], U8, name="p_scales", bufs=2 * NH, align_bytes=64)
+            nc.vector.quantize_mx(
+                out=p_codes[:].bitcast(FP8X4),
+                scales=p_scales[:],
+                in_=p_grouped[unit % 3][:].rearrange("p q t -> p (q t)"),
+            )
+            live["p_codes", unit] = p_codes
+            live["p_scales", unit] = p_scales
+
+        def multiply_pv(b, blocks):
+            for i in blocks:
                 rows = slice(i * P, (i + 1) * P)
-                acc = ps_mx.tile([P, V], F32, tag="mx")
+                acc = psum.tile([P, V], F32, name="acc", tag="bank")
                 for n in range(NH):
                     nc.tensor.matmul_mx(
                         out=acc[:],
-                        lhsT=p_codes[n][:, rows].bitcast(FP8X4),
-                        lhsT_scale=p_scales[n][:, rows],
-                        rhs=vv_codes[:].bitcast(FP8X4),
-                        rhs_scale=vv_scales[:],
+                        lhsT=live["p_codes", b * NH + n][:, rows].bitcast(FP8X4),
+                        lhsT_scale=live["p_scales", b * NH + n][:, rows],
+                        rhs=live["vv_codes", b][:].bitcast(FP8X4),
+                        rhs_scale=live["vv_scales", b][:],
                         start=(n == 0),
                         stop=(n == NH - 1),
                     )
-                result = stores.tile([P, V], F32)
-                nc.scalar.mul(out=result[:], in_=acc[:], mul=1.0 / NH)
-                nc.sync.dma_start(out=out[b, rows, :], in_=result[:])
+                live["acc", b, i] = acc
+
+        def store_out(b, blocks):
+            for i in blocks:
+                result = stores.tile([P, V], F32, name="result")
+                nc.scalar.mul(out=result[:], in_=live["acc", b, i][:], mul=1.0 / NH)
+                nc.sync.dma_start(out=out[b, i * P : (i + 1) * P, :], in_=result[:])
+
+        def unit_stage(unit, stage):
+            if 0 <= unit < UNITS:
+                stage(unit)
+
+        def batch_stage(turn, first, stage):
+            b, rest = divmod(turn - first, NH)
+            if rest == 0 and 0 <= b < B:
+                stage(b)
+
+        for turn in range(-2, UNITS + 4):
+            unit_stage(turn - 1, reciprocal)
+            unit_stage(turn - 1, normalise)
+            unit_stage(turn + 1, copy_qk)
+            unit_stage(turn - 2, group_p)
+            batch_stage(turn, 2, quantise_v)
+            unit_stage(turn, scores)
+            unit_stage(turn, row_max)
+            unit_stage(turn, exponential)
+            unit_stage(turn - 2, quantise_p)
+            batch_stage(turn, 5, lambda b: multiply_pv(b, [0, 1]))
+            batch_stage(turn, 6, lambda b: multiply_pv(b, [2, 3]))
+            batch_stage(turn, 2, lambda b: multiply_vv(b, [0]))
+            batch_stage(turn, 3, lambda b: multiply_vv(b, [1]))
+            batch_stage(turn, 4, lambda b: multiply_vv(b, [2, 3]))
+            batch_stage(turn, 2, lambda b: add_bias(b, [0]))
+            batch_stage(turn, 3, lambda b: add_bias(b, [1]))
+            batch_stage(turn, 4, lambda b: add_bias(b, [2, 3]))
+            batch_stage(turn, 4, quantise_vv)
+            batch_stage(turn, 5, lambda b: store_out(b, [0, 1]))
+            batch_stage(turn, 6, lambda b: store_out(b, [2, 3]))
+            batch_stage(turn, 1, transpose_v)
+            batch_stage(turn, 1, group_v)
+            unit_stage(turn + 2, transpose_qk)
+            unit_stage(turn - 1, transpose_p)

@@ -20,6 +20,8 @@ CHUNKS = S // P
 UNITS = B * NH
 FIRST = [P * i * (i + 1) // 2 for i in range(CHUNKS)]
 WIDTH = P * CHUNKS * (CHUNKS + 1) // 2
+P_FIRST = [0, 256, 512, 1024]
+P_WIDTH = 1536
 SCALE = D ** -0.5
 MASKED = -1.0e30
 
@@ -49,7 +51,7 @@ def tile_interpretablemultiheadattention_pa_t_kernel(tc, qh, kh, v, Wv, bv, out)
                 nc.sync.dma_start(out=k_u[:], in_=kh[n, b].rearrange("(c p) d -> p c d", p=P))
                 k_sb.append(k_u)
             v_b = inputs.tile([P, CHUNKS, H], BF16, name="v%d" % b)
-            nc.sync.dma_start(out=v_b[:], in_=v[b].rearrange("(c p) h -> p c h", p=P))
+            nc.sync.dma_start(out=v_b[:].rearrange("p (u e) h -> p u e h", u=2), in_=v[b].rearrange("(u p e) h -> p u e h", u=2, e=2))
             v_sb.append(v_b)
             if b == 0:
                 nc.sync.dma_start(
@@ -75,11 +77,14 @@ def tile_interpretablemultiheadattention_pa_t_kernel(tc, qh, kh, v, Wv, bv, out)
         nc.vector.tensor_copy(out=mask_bf[:], in_=mask_f32[:])
         ident_f32 = const.tile([P, P], F32)
         make_identity(nc, ident_f32[:])
-        p_grouped = []
+        p_bf16 = []
         for x in range(3):
-            g = const.tile([P, S, PACK], BF16, name="p_grouped%d" % x, align_bytes=64)
-            nc.gpsimd.memset(g[:], 0.0)
-            p_grouped.append(g)
+            g = const.tile([P, P_WIDTH], BF16, name="p_bf%d" % x, align_bytes=64)
+            nc.gpsimd.memset(g[:, 128:256], 0.0)
+            nc.gpsimd.memset(g[:, P_FIRST[2] + 384 : P_FIRST[2] + 512], 0.0)
+            p_bf16.append(g)
+        zeros = const.tile([P, P], F32, align_bytes=64)
+        nc.gpsimd.memset(zeros[:], 0.0)
         w_grouped = const.tile([P, V, PACK], BF16, align_bytes=64)
         w_codes = const.tile([P, V], U32, align_bytes=64)
         w_scales = const.tile([P, V], U8, align_bytes=64)
@@ -249,49 +254,48 @@ def tile_interpretablemultiheadattention_pa_t_kernel(tc, qh, kh, v, Wv, bv, out)
             nc.vector.reciprocal(out=inv_sum[:], in_=live["row_sum", unit][:])
             live["inv_sum", unit] = inv_sum
 
-        P_BANKS = [[3, 0], [2, 1]]
+        P_BANKS = [[2, 3], [0, 1]]
 
         def normalise(unit):
-            p_bf = per_unit.tile([P, WIDTH], BF16, name="p_bf")
             for blocks in P_BANKS:
                 for i in blocks:
-                    cols = slice(FIRST[i], FIRST[i] + (i + 1) * P)
+                    keys = (i + 1) * P
                     nc.gpsimd.tensor_scalar(
-                        out=p_bf[:, cols],
-                        in0=live["e", unit][:, cols],
+                        out=p_bf16[unit % 3][:, P_FIRST[i] : P_FIRST[i] + keys],
+                        in0=live["e", unit][:, FIRST[i] : FIRST[i] + keys],
                         scalar1=live["inv_sum", unit][:, i : i + 1],
                         scalar2=0.0,
                         op0=ALU.mult,
                         op1=ALU.add,
                     )
-            live["p_bf", unit] = p_bf
 
         def transpose_p(unit):
-            p_bf = live["p_bf", unit]
-            for blocks in P_BANKS:
-                pt = psum.tile([P, CHUNKS + 1, P], BF16, name="pt", tag="bank")
-                plane = 0
-                for i in blocks:
-                    for t in range(i + 1):
+            p_words = p_bf16[unit % 3][:].bitcast(F32)
+            for x, blocks in enumerate(P_BANKS):
+                pt = psum.tile([P, 2, 2, P], F32, name="pt", tag="bank")
+                for y, i in enumerate(blocks):
+                    for u in range(2):
+                        first = P_FIRST[i] // 2 + u * P
+                        seen = u <= i // 2
                         nc.tensor.transpose(
-                            pt[:, plane + t, :],
-                            p_bf[:, FIRST[i] + t * P : FIRST[i] + (t + 1) * P],
-                            ident_bf[:],
+                            pt[:, y, u, :],
+                            p_words[:, first : first + P] if seen else zeros[:],
+                            ident_f32[:],
                         )
-                    live["pt", unit, i] = pt[:, plane : plane + i + 1, :]
-                    plane += i + 1
+                live["pt", unit, x] = pt
 
         def group_p(unit):
-            for i in P_BANKS[0]:
-                nc.vector.tensor_copy(
-                    out=p_grouped[unit % 3][:, i * P : (i + 1) * P, 0 : i + 1],
-                    in_=live["pt", unit, i].rearrange("p t q -> p q t"),
-                )
-            for i in P_BANKS[1]:
-                nc.scalar.copy(
-                    out=p_grouped[unit % 3][:, i * P : (i + 1) * P, 0 : i + 1],
-                    in_=live["pt", unit, i].rearrange("p t q -> p q t"),
-                )
+            p_grouped = per_unit.tile([P, S, PACK], BF16, name="p_grouped", align_bytes=64)
+            words = p_grouped[:].rearrange("p q t -> p (q t)").bitcast(F32)
+            nc.vector.tensor_copy(
+                out=words[:, S : 2 * S].rearrange("p (i q u) -> p i q u", i=2, u=2),
+                in_=live["pt", unit, 0][:].rearrange("p i u q -> p i q u"),
+            )
+            nc.scalar.copy(
+                out=words[:, 0:S].rearrange("p (i q u) -> p i q u", i=2, u=2),
+                in_=live["pt", unit, 1][:].rearrange("p i u q -> p i q u"),
+            )
+            live["p_grouped", unit] = p_grouped
 
         def quantise_p(unit):
             p_codes = per_unit.tile([P, S], U32, name="p_codes", bufs=2 * NH, align_bytes=64)
@@ -299,7 +303,7 @@ def tile_interpretablemultiheadattention_pa_t_kernel(tc, qh, kh, v, Wv, bv, out)
             nc.vector.quantize_mx(
                 out=p_codes[:].bitcast(FP8X4),
                 scales=p_scales[:],
-                in_=p_grouped[unit % 3][:].rearrange("p q t -> p (q t)"),
+                in_=live["p_grouped", unit][:].rearrange("p q t -> p (q t)"),
             )
             live["p_codes", unit] = p_codes
             live["p_scales", unit] = p_scales

@@ -36,7 +36,8 @@ def tile_interpretablemultiheadattention_pa_t_kernel(tc, qh, kh, v, Wv, bv, out)
         per_unit = ctx.enter_context(tc.tile_pool(name="per_unit", bufs=3))
         per_batch = ctx.enter_context(tc.tile_pool(name="per_batch", bufs=2))
         stores = ctx.enter_context(tc.tile_pool(name="stores", bufs=4))
-        psum = ctx.enter_context(tc.psum_pool(name="psum", bufs=8))
+        psum_low = ctx.enter_context(tc.psum_pool(name="psum_low", bufs=1))
+        psum = ctx.enter_context(tc.psum_pool(name="psum", bufs=7))
         ctx.enter_context(tc.manual_schedule())
 
         v_sb, q_sb, k_sb = [], [], []
@@ -85,6 +86,9 @@ def tile_interpretablemultiheadattention_pa_t_kernel(tc, qh, kh, v, Wv, bv, out)
             p_bf16.append(g)
         zeros = const.tile([P, P], F32, align_bytes=64)
         nc.gpsimd.memset(zeros[:], 0.0)
+        low = psum_low.tile([P, 2, 2, P], F32, name="low")
+        for i in range(2):
+            nc.tensor.transpose(low[:, 1, i, :], zeros[:], ident_f32[:])
         w_grouped = const.tile([P, V, PACK], BF16, align_bytes=64)
         w_codes = const.tile([P, V], U32, align_bytes=64)
         w_scales = const.tile([P, V], U8, align_bytes=64)
@@ -271,29 +275,26 @@ def tile_interpretablemultiheadattention_pa_t_kernel(tc, qh, kh, v, Wv, bv, out)
 
         def transpose_p(unit):
             p_words = p_bf16[unit % 3][:].bitcast(F32)
-            for x, blocks in enumerate(P_BANKS):
-                pt = psum.tile([P, 2, 2, P], F32, name="pt", tag="bank")
-                for y, i in enumerate(blocks):
-                    for u in range(2):
-                        first = P_FIRST[i] // 2 + u * P
-                        seen = u <= i // 2
-                        nc.tensor.transpose(
-                            pt[:, y, u, :],
-                            p_words[:, first : first + P] if seen else zeros[:],
-                            ident_f32[:],
-                        )
-                live["pt", unit, x] = pt
+            pt = psum.tile([P, 2, 2, P], F32, name="pt", tag="bank")
+            for y, i in enumerate(P_BANKS[0]):
+                for u in range(2):
+                    first = P_FIRST[i] // 2 + u * P
+                    nc.tensor.transpose(pt[:, y, u, :], p_words[:, first : first + P], ident_f32[:])
+            live["pt", unit] = pt
+            for i in P_BANKS[1]:
+                first = P_FIRST[i] // 2
+                nc.tensor.transpose(low[:, 0, i, :], p_words[:, first : first + P], ident_f32[:])
 
         def group_p(unit):
             p_grouped = per_unit.tile([P, S, PACK], BF16, name="p_grouped", align_bytes=64)
             words = p_grouped[:].rearrange("p q t -> p (q t)").bitcast(F32)
             nc.vector.tensor_copy(
                 out=words[:, S : 2 * S].rearrange("p (i q u) -> p i q u", i=2, u=2),
-                in_=live["pt", unit, 0][:].rearrange("p i u q -> p i q u"),
+                in_=live["pt", unit][:].rearrange("p i u q -> p i q u"),
             )
             nc.scalar.copy(
                 out=words[:, 0:S].rearrange("p (i q u) -> p i q u", i=2, u=2),
-                in_=live["pt", unit, 1][:].rearrange("p i u q -> p i q u"),
+                in_=low[:].rearrange("p u i q -> p i q u"),
             )
             live["p_grouped", unit] = p_grouped
 
@@ -360,7 +361,7 @@ def tile_interpretablemultiheadattention_pa_t_kernel(tc, qh, kh, v, Wv, bv, out)
             batch_stage(turn, 4, quantise_vv)
             batch_stage(turn, 5, lambda b: store_out(b, [0, 1]))
             batch_stage(turn, 6, lambda b: store_out(b, [2, 3]))
+            unit_stage(turn + 2, transpose_qk)
             batch_stage(turn, 1, transpose_v)
             batch_stage(turn, 1, group_v)
-            unit_stage(turn + 2, transpose_qk)
             unit_stage(turn - 1, transpose_p)

@@ -9,6 +9,7 @@ U32 = mybir.dt.uint32
 U8 = mybir.dt.uint8
 FP8X4 = mybir.dt.float8_e4m3fn_x4
 ALU = mybir.AluOpType
+AX = mybir.AxisListType
 ACT = mybir.ActivationFunctionType
 
 P = 128
@@ -35,7 +36,7 @@ def tile_interpretablemultiheadattention_pa_t_kernel(tc, qh, kh, v, Wv, bv, out)
         inputs = ctx.enter_context(tc.tile_pool(name="inputs", bufs=1))
         per_unit = ctx.enter_context(tc.tile_pool(name="per_unit", bufs=3))
         per_batch = ctx.enter_context(tc.tile_pool(name="per_batch", bufs=2))
-        stores = ctx.enter_context(tc.tile_pool(name="stores", bufs=4))
+        stores = ctx.enter_context(tc.tile_pool(name="stores", bufs=8))
         psum_low = ctx.enter_context(tc.psum_pool(name="psum_low", bufs=1))
         psum = ctx.enter_context(tc.psum_pool(name="psum", bufs=7))
         ctx.enter_context(tc.manual_schedule())
@@ -43,23 +44,32 @@ def tile_interpretablemultiheadattention_pa_t_kernel(tc, qh, kh, v, Wv, bv, out)
         v_sb, q_sb, k_sb = [], [], []
         w_raw = const.tile([P, PACK, V], BF16)
         bias = const.tile([P, V], BF16)
-        for b in range(B):
-            for n in range(NH):
-                q_u = inputs.tile([P, CHUNKS, D], BF16, name="q%d_%d" % (b, n))
-                nc.sync.dma_start(out=q_u[:], in_=qh[n, b].rearrange("(c p) d -> p c d", p=P))
-                q_sb.append(q_u)
-                k_u = inputs.tile([P, CHUNKS, D], BF16, name="k%d_%d" % (b, n))
-                nc.sync.dma_start(out=k_u[:], in_=kh[n, b].rearrange("(c p) d -> p c d", p=P))
-                k_sb.append(k_u)
+
+        def load_v(b):
             v_b = inputs.tile([P, CHUNKS, H], BF16, name="v%d" % b)
-            nc.sync.dma_start(out=v_b[:].rearrange("p (u e) h -> p u e h", u=2), in_=v[b].rearrange("(u p e) h -> p u e h", u=2, e=2))
+            nc.sync.dma_start(
+                out=v_b[:].rearrange("p (u e) h -> p u e h", u=2),
+                in_=v[b].rearrange("(u p e) h -> p u e h", u=2, e=2),
+            )
             v_sb.append(v_b)
-            if b == 0:
+
+        for unit in range(UNITS):
+            b, n = divmod(unit, NH)
+            q_u = inputs.tile([P, CHUNKS, D], BF16, name="q%d" % unit)
+            nc.sync.dma_start(out=q_u[:], in_=qh[n, b].rearrange("(c p) d -> p c d", p=P))
+            q_sb.append(q_u)
+            k_u = inputs.tile([P, CHUNKS, D], BF16, name="k%d" % unit)
+            nc.sync.dma_start(out=k_u[:], in_=kh[n, b].rearrange("(c p) d -> p c d", p=P))
+            k_sb.append(k_u)
+            if unit == 2:
+                load_v(0)
                 nc.sync.dma_start(
                     out=w_raw[:].rearrange("q (u e) c -> q u e c", u=2),
                     in_=Wv.rearrange("(u q e) c -> q u e c", u=2, e=2),
                 )
                 nc.sync.dma_start(out=bias[:], in_=bv.partition_broadcast(P))
+            if unit % NH == 2 and b < B - 1:
+                load_v(b + 1)
 
         ident_bf = const.tile([P, P], BF16)
         make_identity(nc, ident_bf[:])
@@ -87,39 +97,48 @@ def tile_interpretablemultiheadattention_pa_t_kernel(tc, qh, kh, v, Wv, bv, out)
         zeros = const.tile([P, P], F32, align_bytes=64)
         nc.gpsimd.memset(zeros[:], 0.0)
         low = psum_low.tile([P, 2, 2, P], F32, name="low")
-        for i in range(2):
-            nc.tensor.transpose(low[:, 1, i, :], zeros[:], ident_f32[:])
+
+        def clear_low():
+            for i in range(2):
+                nc.tensor.transpose(low[:, 1, i, :], zeros[:], ident_f32[:])
+
         w_grouped = const.tile([P, V, PACK], BF16, align_bytes=64)
         w_codes = const.tile([P, V], U32, align_bytes=64)
         w_scales = const.tile([P, V], U8, align_bytes=64)
 
         live = {}
 
-        def transpose_v(b):
+        def transpose_v(b, half):
             v_words = v_sb[b][:].rearrange("p c h -> p (c h)").bitcast(F32)
-            for half in range(2):
-                vt = psum.tile([P, 2, 2, P], F32, name="vt", tag="bank")
-                for c in range(2):
-                    for u in range(2):
-                        first = (2 * half + c) * (H // 2) + u * P
-                        nc.tensor.transpose(
-                            vt[:, c, u, :], v_words[:, first : first + P], ident_f32[:]
-                        )
-                live["vt", b, half] = vt
+            vt = psum.tile([P, 2, 2, P], F32, name="vt", tag="bank")
+            for c in range(2):
+                for u in range(2):
+                    first = (2 * half + c) * (H // 2) + u * P
+                    nc.tensor.transpose(vt[:, c, u, :], v_words[:, first : first + P], ident_f32[:])
+            live["vt", b, half] = vt
 
-        def group_v(b):
-            v_grouped = per_batch.tile([P, S, PACK], BF16, name="v_grouped", align_bytes=64)
-            words = v_grouped[:].rearrange("p r t -> p (r t)").bitcast(F32)
-            for half in range(2):
-                nc.scalar.copy(
-                    out=words[:, half * S : (half + 1) * S].rearrange(
-                        "p (c r u) -> p c r u", c=2, u=2
-                    ),
-                    in_=live["vt", b, half][:].rearrange("p c u r -> p c r u"),
+        def group_v(b, half):
+            if half == 0:
+                live["v_grouped", b] = per_batch.tile(
+                    [P, S, PACK], BF16, name="v_grouped", align_bytes=64
                 )
-            live["v_grouped", b] = v_grouped
-            if b == 0:
-                nc.vector.tensor_copy(out=w_grouped[:], in_=w_raw[:].rearrange("q t c -> q c t"))
+            words = live["v_grouped", b][:].rearrange("p r t -> p (r t)").bitcast(F32)
+            nc.scalar.copy(
+                out=words[:, half * S : (half + 1) * S].rearrange(
+                    "p (c r u) -> p c r u", c=2, u=2
+                ),
+                in_=live["vt", b, half][:].rearrange("p c u r -> p c r u"),
+            )
+
+        def group_w():
+            nc.vector.tensor_copy(out=w_grouped[:], in_=w_raw[:].rearrange("q t c -> q c t"))
+
+        def quantise_w():
+            nc.vector.quantize_mx(
+                out=w_codes[:].bitcast(FP8X4),
+                scales=w_scales[:],
+                in_=w_grouped[:].rearrange("q c t -> q (c t)"),
+            )
 
         def quantise_v(b):
             v_codes = per_batch.tile([P, S], U32, name="v_codes", align_bytes=64)
@@ -131,12 +150,6 @@ def tile_interpretablemultiheadattention_pa_t_kernel(tc, qh, kh, v, Wv, bv, out)
             )
             live["v_codes", b] = v_codes
             live["v_scales", b] = v_scales
-            if b == 0:
-                nc.vector.quantize_mx(
-                    out=w_codes[:].bitcast(FP8X4),
-                    scales=w_scales[:],
-                    in_=w_grouped[:].rearrange("q c t -> q (c t)"),
-                )
 
         def multiply_vv(b, pieces):
             for w in pieces:
@@ -261,17 +274,21 @@ def tile_interpretablemultiheadattention_pa_t_kernel(tc, qh, kh, v, Wv, bv, out)
         P_BANKS = [[2, 3], [0, 1]]
 
         def normalise(unit):
+            last = unit == UNITS - 1
             for blocks in P_BANKS:
                 for i in blocks:
                     keys = (i + 1) * P
-                    nc.gpsimd.tensor_scalar(
-                        out=p_bf16[unit % 3][:, P_FIRST[i] : P_FIRST[i] + keys],
-                        in0=live["e", unit][:, FIRST[i] : FIRST[i] + keys],
-                        scalar1=live["inv_sum", unit][:, i : i + 1],
-                        scalar2=0.0,
-                        op0=ALU.mult,
-                        op1=ALU.add,
-                    )
+                    p_i = p_bf16[unit % 3][:, P_FIRST[i] : P_FIRST[i] + keys]
+                    e_i = live["e", unit][:, FIRST[i] : FIRST[i] + keys]
+                    inv_i = live["inv_sum", unit][:, i : i + 1]
+                    if last and i % 2 == 1:
+                        nc.vector.tensor_scalar_mul(out=p_i, in0=e_i, scalar1=inv_i)
+                    elif last:
+                        nc.scalar.activation(out=p_i, in_=e_i, func=ACT.Copy, scale=inv_i)
+                    else:
+                        nc.gpsimd.tensor_scalar(
+                            out=p_i, in0=e_i, scalar1=inv_i, scalar2=0.0, op0=ALU.mult, op1=ALU.add
+                        )
 
         def transpose_p(unit):
             p_words = p_bf16[unit % 3][:].bitcast(F32)
@@ -298,24 +315,28 @@ def tile_interpretablemultiheadattention_pa_t_kernel(tc, qh, kh, v, Wv, bv, out)
             )
             live["p_grouped", unit] = p_grouped
 
-        def quantise_p(unit):
+        def quantise_p(unit, parts=1):
             p_codes = per_unit.tile([P, S], U32, name="p_codes", bufs=2 * NH, align_bytes=64)
             p_scales = per_unit.tile([P, S], U8, name="p_scales", bufs=2 * NH, align_bytes=64)
-            nc.vector.quantize_mx(
-                out=p_codes[:].bitcast(FP8X4),
-                scales=p_scales[:],
-                in_=live["p_grouped", unit][:].rearrange("p q t -> p (q t)"),
-            )
+            n = S // parts
+            for x in range(parts):
+                rows = slice(x * n, (x + 1) * n)
+                nc.vector.quantize_mx(
+                    out=p_codes[:, rows].bitcast(FP8X4),
+                    scales=p_scales[:, rows],
+                    in_=live["p_grouped", unit][:, rows, :].rearrange("p q t -> p (q t)"),
+                )
             live["p_codes", unit] = p_codes
             live["p_scales", unit] = p_scales
 
-        def multiply_pv(b, blocks):
+        def multiply_pv(b, blocks, heads=range(NH), ):
             for i in blocks:
                 rows = slice(i * P, (i + 1) * P)
-                acc = psum.tile([P, V], F32, name="acc", tag="bank")
-                for n in range(NH):
+                if 0 in heads:
+                    live["acc", b, i] = psum.tile([P, V], F32, name="acc", tag="bank")
+                for n in heads:
                     nc.tensor.matmul_mx(
-                        out=acc[:],
+                        out=live["acc", b, i][:],
                         lhsT=live["p_codes", b * NH + n][:, rows].bitcast(FP8X4),
                         lhsT_scale=live["p_scales", b * NH + n][:, rows],
                         rhs=live["vv_codes", b][:].bitcast(FP8X4),
@@ -323,12 +344,14 @@ def tile_interpretablemultiheadattention_pa_t_kernel(tc, qh, kh, v, Wv, bv, out)
                         start=(n == 0),
                         stop=(n == NH - 1),
                     )
-                live["acc", b, i] = acc
 
-        def store_out(b, blocks):
+        def store_out(b, blocks, vector=()):
             for i in blocks:
                 result = stores.tile([P, V], F32, name="result")
-                nc.scalar.mul(out=result[:], in_=live["acc", b, i][:], mul=1.0 / NH)
+                if i in vector:
+                    nc.vector.tensor_scalar_mul(out=result[:], in0=live["acc", b, i][:], scalar1=1.0 / NH)
+                else:
+                    nc.scalar.mul(out=result[:], in_=live["acc", b, i][:], mul=1.0 / NH)
                 nc.sync.dma_start(out=out[b, i * P : (i + 1) * P, :], in_=result[:])
 
         def unit_stage(unit, stage):
@@ -340,28 +363,57 @@ def tile_interpretablemultiheadattention_pa_t_kernel(tc, qh, kh, v, Wv, bv, out)
             if rest == 0 and 0 <= b < B:
                 stage(b)
 
-        for turn in range(-2, UNITS + 4):
+        SHIFT = [0,0,0,0,0,0,-1,-2]
+        def vv_turn(turn, first, stage):
+            for b in range(B):
+                if turn == NH * b + first + SHIFT[b]:
+                    stage(b)
+
+        for turn in range(-2, UNITS):
             unit_stage(turn - 1, reciprocal)
             unit_stage(turn - 1, normalise)
+            batch_stage(turn, 6, lambda b: store_out(b, [0]))
+            batch_stage(turn, 7, lambda b: store_out(b, [1]))
+            batch_stage(turn, 8, lambda b: store_out(b, [2,3]))
             unit_stage(turn + 1, copy_qk)
             unit_stage(turn - 2, group_p)
-            batch_stage(turn, 2, quantise_v)
+            vv_turn(turn, 0, lambda b: group_v(b, 0))
+            vv_turn(turn, 1, lambda b: group_v(b, 1))
             unit_stage(turn, scores)
+            if turn == 0:
+                clear_low()
             unit_stage(turn, row_max)
             unit_stage(turn, exponential)
+            if turn == 1:
+                group_w()
+                quantise_w()
             unit_stage(turn - 2, quantise_p)
-            batch_stage(turn, 5, lambda b: multiply_pv(b, [0, 1]))
-            batch_stage(turn, 6, lambda b: multiply_pv(b, [2, 3]))
-            batch_stage(turn, 2, lambda b: multiply_vv(b, [0]))
-            batch_stage(turn, 3, lambda b: multiply_vv(b, [1]))
-            batch_stage(turn, 4, lambda b: multiply_vv(b, [2, 3]))
-            batch_stage(turn, 2, lambda b: add_bias(b, [0]))
-            batch_stage(turn, 3, lambda b: add_bias(b, [1]))
-            batch_stage(turn, 4, lambda b: add_bias(b, [2, 3]))
-            batch_stage(turn, 4, quantise_vv)
-            batch_stage(turn, 5, lambda b: store_out(b, [0, 1]))
-            batch_stage(turn, 6, lambda b: store_out(b, [2, 3]))
+            vv_turn(turn, 1, quantise_v)
+            vv_turn(turn, 4, quantise_vv)
+            batch_stage(turn, 5, lambda b: multiply_pv(b, [0]))
+            batch_stage(turn, 6, lambda b: multiply_pv(b, [1]))
+            batch_stage(turn, 7, lambda b: multiply_pv(b, [2,3]))
+            vv_turn(turn, 2, lambda b: multiply_vv(b, [0, 1]))
+            vv_turn(turn, 3, lambda b: multiply_vv(b, [2, 3]))
+            vv_turn(turn, 2, lambda b: add_bias(b, [0, 1]))
+            vv_turn(turn, 3, lambda b: add_bias(b, [2, 3]))
             unit_stage(turn + 2, transpose_qk)
-            batch_stage(turn, 1, transpose_v)
-            batch_stage(turn, 1, group_v)
+            vv_turn(turn, -1, lambda b: transpose_v(b, 0))
+            vv_turn(turn, 0, lambda b: transpose_v(b, 1))
             unit_stage(turn - 1, transpose_p)
+        b = B - 1
+        u = UNITS - 1
+        reciprocal(u)
+        normalise(u)
+        group_p(u - 1)
+        quantise_p(u - 1)
+        multiply_pv(b - 1, [1,2,3])
+        transpose_p(u)
+        group_p(u)
+        store_out(b - 1, [0, 1])
+        multiply_pv(b, [0, 1, 2], heads=[0, 1])
+        quantise_p(u, parts=2)
+        store_out(b - 1, [2, 3], vector=[2])
+        multiply_pv(b, [3], heads=[0, 1])
+        multiply_pv(b, [0, 1, 2, 3], heads=[2])
+        store_out(b, [0, 1, 2, 3], vector=[0, 2])

@@ -15,6 +15,7 @@ ACT = mybir.ActivationFunctionType
 P = 128
 PACK = 4
 NH, B, S, D = 3, 8, 512, 128
+AHEAD = 5
 H = 512
 V = 512
 CHUNKS = S // P
@@ -44,6 +45,10 @@ def tile_interpretablemultiheadattention_pa_t_kernel(tc, qh, kh, v, Wv, bv, out)
         v_sb, q_sb, k_sb = [], [], []
         w_raw = const.tile([P, PACK, V], BF16)
         bias = const.tile([P, V], BF16)
+        bias_row = const.tile([P, V], BF16)
+        nc.gpsimd.memset(bias_row[:], 0.0)
+        ones = const.tile([P, P], BF16)
+        nc.gpsimd.memset(ones[:], 1.0)
 
         def load_v(b):
             v_b = inputs.tile([P, CHUNKS, H], BF16, name="v%d" % b)
@@ -53,7 +58,7 @@ def tile_interpretablemultiheadattention_pa_t_kernel(tc, qh, kh, v, Wv, bv, out)
             )
             v_sb.append(v_b)
 
-        for unit in range(UNITS):
+        def load(unit):
             b, n = divmod(unit, NH)
             q_u = inputs.tile([P, CHUNKS, D], BF16, name="q%d" % unit)
             nc.sync.dma_start(out=q_u[:], in_=qh[n, b].rearrange("(c p) d -> p c d", p=P))
@@ -63,13 +68,18 @@ def tile_interpretablemultiheadattention_pa_t_kernel(tc, qh, kh, v, Wv, bv, out)
             k_sb.append(k_u)
             if unit == 2:
                 load_v(0)
+            if unit == 2:
                 nc.sync.dma_start(
                     out=w_raw[:].rearrange("q (u e) c -> q u e c", u=2),
                     in_=Wv.rearrange("(u q e) c -> q u e c", u=2, e=2),
                 )
-                nc.sync.dma_start(out=bias[:], in_=bv.partition_broadcast(P))
-            if unit % NH == 2 and b < B - 1:
-                load_v(b + 1)
+            if unit == 2:
+                nc.sync.dma_start(out=bias_row[0:1, :], in_=bv.unsqueeze(0))
+            if n == 1 and b > 0:
+                load_v(b)
+
+        for unit in range(AHEAD - 1):
+            load(unit)
 
         ident_bf = const.tile([P, P], BF16)
         make_identity(nc, ident_bf[:])
@@ -129,6 +139,11 @@ def tile_interpretablemultiheadattention_pa_t_kernel(tc, qh, kh, v, Wv, bv, out)
                 ),
                 in_=live["vt", b, half][:].rearrange("p c u r -> p c r u"),
             )
+
+        def spread_bias():
+            spread = psum.tile([P, V], F32, name="spread", tag="bank")
+            nc.tensor.matmul(out=spread[:], lhsT=ones[:], rhs=bias_row[:], start=True, stop=True)
+            nc.scalar.copy(out=bias[:], in_=spread[:])
 
         def group_w():
             nc.vector.tensor_copy(out=w_grouped[:], in_=w_raw[:].rearrange("q t c -> q c t"))
@@ -305,7 +320,7 @@ def tile_interpretablemultiheadattention_pa_t_kernel(tc, qh, kh, v, Wv, bv, out)
         def group_p(unit):
             p_grouped = per_unit.tile([P, S, PACK], BF16, name="p_grouped", align_bytes=64)
             words = p_grouped[:].rearrange("p q t -> p (q t)").bitcast(F32)
-            nc.vector.tensor_copy(
+            (nc.scalar.copy if unit % 3 == 0 else nc.vector.tensor_copy)(
                 out=words[:, S : 2 * S].rearrange("p (i q u) -> p i q u", i=2, u=2),
                 in_=live["pt", unit][:].rearrange("p i u q -> p i q u"),
             )
@@ -363,18 +378,24 @@ def tile_interpretablemultiheadattention_pa_t_kernel(tc, qh, kh, v, Wv, bv, out)
             if rest == 0 and 0 <= b < B:
                 stage(b)
 
-        SHIFT = [0,0,0,0,0,0,-1,-2]
+        SHIFT = [1,0,0,0,0,0,-1,-2]
         def vv_turn(turn, first, stage):
             for b in range(B):
                 if turn == NH * b + first + SHIFT[b]:
                     stage(b)
 
+        def pv_turn(turn, stage):
+            b, third = divmod(turn - 5, NH)
+            blocks = PV0[third] if b == 0 else [[0], [1], [2, 3]][third]
+            if 0 <= b < B and blocks:
+                stage(b, blocks)
+
+        PV0 = [[], [0, 1], [2, 3]]
         for turn in range(-2, UNITS):
+            unit_stage(turn + AHEAD + 1, load)
             unit_stage(turn - 1, reciprocal)
             unit_stage(turn - 1, normalise)
-            batch_stage(turn, 6, lambda b: store_out(b, [0]))
-            batch_stage(turn, 7, lambda b: store_out(b, [1]))
-            batch_stage(turn, 8, lambda b: store_out(b, [2,3]))
+            pv_turn(turn - 1, store_out)
             unit_stage(turn + 1, copy_qk)
             unit_stage(turn - 2, group_p)
             vv_turn(turn, 0, lambda b: group_v(b, 0))
@@ -385,14 +406,14 @@ def tile_interpretablemultiheadattention_pa_t_kernel(tc, qh, kh, v, Wv, bv, out)
             unit_stage(turn, row_max)
             unit_stage(turn, exponential)
             if turn == 1:
+                spread_bias()
                 group_w()
+            if turn == 1:
                 quantise_w()
             unit_stage(turn - 2, quantise_p)
             vv_turn(turn, 1, quantise_v)
             vv_turn(turn, 4, quantise_vv)
-            batch_stage(turn, 5, lambda b: multiply_pv(b, [0]))
-            batch_stage(turn, 6, lambda b: multiply_pv(b, [1]))
-            batch_stage(turn, 7, lambda b: multiply_pv(b, [2,3]))
+            pv_turn(turn, multiply_pv)
             vv_turn(turn, 2, lambda b: multiply_vv(b, [0, 1]))
             vv_turn(turn, 3, lambda b: multiply_vv(b, [2, 3]))
             vv_turn(turn, 2, lambda b: add_bias(b, [0, 1]))

@@ -210,10 +210,15 @@ def tile_interpretablemultiheadattention_pa_t_kernel(tc, qh, kh, v, Wv, bv, out)
 
         def transpose_qk(unit):
             qk_ps = psum.tile([P, 2, S], BF16, name="qk_ps", tag="bank")
-            for c in range(CHUNKS):
-                nc.tensor.transpose(qk_ps[:, 0, c * P : (c + 1) * P], q_sb[unit][:, c, :], ident_bf[:])
-            for c in range(CHUNKS):
-                nc.tensor.transpose(qk_ps[:, 1, c * P : (c + 1) * P], k_sb[unit][:, c, :], ident_bf[:])
+            for x, blocks in enumerate([q_sb[unit], k_sb[unit]]):
+                for c in range(CHUNKS):
+                    turned = qk_ps[:, x, c * P : (c + 1) * P]
+                    if x == 0:
+                        nc.tensor.matmul(
+                            out=turned, lhsT=blocks[:, c, :], rhs=ident_bf[:], start=True, stop=True
+                        )
+                    else:
+                        nc.tensor.transpose(turned, blocks[:, c, :], ident_bf[:])
             live["qk_ps", unit] = qk_ps
 
         def copy_qk(unit):
@@ -426,15 +431,15 @@ def tile_interpretablemultiheadattention_pa_t_kernel(tc, qh, kh, v, Wv, bv, out)
         u = UNITS - 1
         reciprocal(u)
         normalise(u)
+        multiply_pv(b - 1, [1])
         group_p(u - 1)
         quantise_p(u - 1)
-        multiply_pv(b - 1, [1,2,3])
         transpose_p(u)
-        group_p(u)
         store_out(b - 1, [0, 1])
-        multiply_pv(b, [0, 1, 2], heads=[0, 1])
+        multiply_pv(b - 1, [2, 3])
+        group_p(u)
+        store_out(b - 1, [2, 3], vector=[3])
         quantise_p(u, parts=2)
-        store_out(b - 1, [2, 3], vector=[2])
-        multiply_pv(b, [3], heads=[0, 1])
-        multiply_pv(b, [0, 1, 2, 3], heads=[2])
-        store_out(b, [0, 1, 2, 3], vector=[0, 2])
+        for i in range(CHUNKS):
+            multiply_pv(b, [i])
+            store_out(b, [i], vector=[0, 2])

@@ -301,7 +301,7 @@ def tile_interpretablemultiheadattention_pa_t_kernel(tc, qh, kh, v, Wv, bv, out)
                     p_i = p_bf16[unit % 3][:, P_FIRST[i] : P_FIRST[i] + keys]
                     e_i = live["e", unit][:, FIRST[i] : FIRST[i] + keys]
                     inv_i = live["inv_sum", unit][:, i : i + 1]
-                    if last and i % 2 == 1:
+                    if i == 1 or (last and i == 3):
                         nc.vector.tensor_scalar_mul(out=p_i, in0=e_i, scalar1=inv_i)
                     elif last:
                         nc.scalar.activation(out=p_i, in_=e_i, func=ACT.Copy, scale=inv_i)

@@ -301,7 +301,7 @@ def tile_interpretablemultiheadattention_pa_t_kernel(tc, qh, kh, v, Wv, bv, out)
                     p_i = p_bf16[unit % 3][:, P_FIRST[i] : P_FIRST[i] + keys]
                     e_i = live["e", unit][:, FIRST[i] : FIRST[i] + keys]
                     inv_i = live["inv_sum", unit][:, i : i + 1]
-                    if i == 1 or (last and i == 3):
+                    if (i % 2 == 1) if last else (i < 2):
                         nc.vector.tensor_scalar_mul(out=p_i, in0=e_i, scalar1=inv_i)
                     elif last:
                         nc.scalar.activation(out=p_i, in_=e_i, func=ACT.Copy, scale=inv_i)
@@ -325,7 +325,7 @@ def tile_interpretablemultiheadattention_pa_t_kernel(tc, qh, kh, v, Wv, bv, out)
         def group_p(unit):
             p_grouped = per_unit.tile([P, S, PACK], BF16, name="p_grouped", align_bytes=64)
             words = p_grouped[:].rearrange("p q t -> p (q t)").bitcast(F32)
-            (nc.scalar.copy if unit % 3 == 0 else nc.vector.tensor_copy)(
+            (nc.scalar.copy if unit % 3 != 1 and unit < UNITS - 1 else nc.vector.tensor_copy)(
                 out=words[:, S : 2 * S].rearrange("p (i q u) -> p i q u", i=2, u=2),
                 in_=live["pt", unit][:].rearrange("p i u q -> p i q u"),
             )
@@ -435,11 +435,11 @@ def tile_interpretablemultiheadattention_pa_t_kernel(tc, qh, kh, v, Wv, bv, out)
         group_p(u - 1)
         quantise_p(u - 1)
         transpose_p(u)
-        store_out(b - 1, [0, 1])
+        store_out(b - 1, [0])
         multiply_pv(b - 1, [2, 3])
         group_p(u)
-        store_out(b - 1, [2, 3], vector=[3])
         quantise_p(u, parts=2)
+        store_out(b - 1, [1,2,3], vector=[2])
         for i in range(CHUNKS):
             multiply_pv(b, [i])
             store_out(b, [i], vector=[0, 2])

@@ -66,14 +66,12 @@ def tile_interpretablemultiheadattention_pa_t_kernel(tc, qh, kh, v, Wv, bv, out)
             k_u = inputs.tile([P, CHUNKS, D], BF16, name="k%d" % unit)
             nc.sync.dma_start(out=k_u[:], in_=kh[n, b].rearrange("(c p) d -> p c d", p=P))
             k_sb.append(k_u)
-            if unit == 2:
+            if unit == NH - 1:
                 load_v(0)
-            if unit == 2:
                 nc.sync.dma_start(
                     out=w_raw[:].rearrange("q (u e) c -> q u e c", u=2),
                     in_=Wv.rearrange("(u q e) c -> q u e c", u=2, e=2),
                 )
-            if unit == 2:
                 nc.sync.dma_start(out=bias_row[0:1, :], in_=bv.unsqueeze(0))
             if n == 1 and b > 0:
                 load_v(b)
@@ -349,14 +347,13 @@ def tile_interpretablemultiheadattention_pa_t_kernel(tc, qh, kh, v, Wv, bv, out)
             live["p_codes", unit] = p_codes
             live["p_scales", unit] = p_scales
 
-        def multiply_pv(b, blocks, heads=range(NH), ):
+        def multiply_pv(b, blocks):
             for i in blocks:
                 rows = slice(i * P, (i + 1) * P)
-                if 0 in heads:
-                    live["acc", b, i] = psum.tile([P, V], F32, name="acc", tag="bank")
-                for n in heads:
+                acc = psum.tile([P, V], F32, name="acc", tag="bank")
+                for n in range(NH):
                     nc.tensor.matmul_mx(
-                        out=live["acc", b, i][:],
+                        out=acc[:],
                         lhsT=live["p_codes", b * NH + n][:, rows].bitcast(FP8X4),
                         lhsT_scale=live["p_scales", b * NH + n][:, rows],
                         rhs=live["vv_codes", b][:].bitcast(FP8X4),
@@ -364,6 +361,7 @@ def tile_interpretablemultiheadattention_pa_t_kernel(tc, qh, kh, v, Wv, bv, out)
                         start=(n == 0),
                         stop=(n == NH - 1),
                     )
+                live["acc", b, i] = acc
 
         def store_out(b, blocks, vector=()):
             for i in blocks:
@@ -378,20 +376,14 @@ def tile_interpretablemultiheadattention_pa_t_kernel(tc, qh, kh, v, Wv, bv, out)
             if 0 <= unit < UNITS:
                 stage(unit)
 
-        def batch_stage(turn, first, stage):
-            b, rest = divmod(turn - first, NH)
-            if rest == 0 and 0 <= b < B:
-                stage(b)
-
-        SHIFT = [1,0,0,0,0,0,-1,-2]
-        def vv_turn(turn, first, stage):
+        def vv_turn(turn, step, stage):
             for b in range(B):
-                if turn == NH * b + first + SHIFT[b]:
+                if turn == max(2 * b, NH * (b - 1)) + step:
                     stage(b)
 
         def pv_turn(turn, stage):
             b, third = divmod(turn - 5, NH)
-            blocks = PV0[third] if b == 0 else [[0], [1], [2, 3]][third]
+            blocks = PV0[third] if b == 0 else [[0, 1], [2], [3]][third]
             if 0 <= b < B and blocks:
                 stage(b, blocks)
 
@@ -403,8 +395,8 @@ def tile_interpretablemultiheadattention_pa_t_kernel(tc, qh, kh, v, Wv, bv, out)
             pv_turn(turn - 1, store_out)
             unit_stage(turn + 1, copy_qk)
             unit_stage(turn - 2, group_p)
-            vv_turn(turn, 0, lambda b: group_v(b, 0))
-            vv_turn(turn, 1, lambda b: group_v(b, 1))
+            vv_turn(turn, 1, lambda b: group_v(b, 0))
+            vv_turn(turn, 2, lambda b: group_v(b, 1))
             unit_stage(turn, scores)
             if turn == 0:
                 clear_low()
@@ -413,33 +405,32 @@ def tile_interpretablemultiheadattention_pa_t_kernel(tc, qh, kh, v, Wv, bv, out)
             if turn == 1:
                 spread_bias()
                 group_w()
-            if turn == 1:
                 quantise_w()
             unit_stage(turn - 2, quantise_p)
-            vv_turn(turn, 1, quantise_v)
-            vv_turn(turn, 4, quantise_vv)
+            vv_turn(turn, 2, quantise_v)
+            vv_turn(turn, 5, quantise_vv)
             pv_turn(turn, multiply_pv)
-            vv_turn(turn, 2, lambda b: multiply_vv(b, [0, 1]))
-            vv_turn(turn, 3, lambda b: multiply_vv(b, [2, 3]))
-            vv_turn(turn, 2, lambda b: add_bias(b, [0, 1]))
-            vv_turn(turn, 3, lambda b: add_bias(b, [2, 3]))
+            vv_turn(turn, 3, lambda b: multiply_vv(b, [0, 1]))
+            vv_turn(turn, 4, lambda b: multiply_vv(b, [2, 3]))
+            vv_turn(turn, 3, lambda b: add_bias(b, [0, 1]))
+            vv_turn(turn, 4, lambda b: add_bias(b, [2, 3]))
             unit_stage(turn + 2, transpose_qk)
-            vv_turn(turn, -1, lambda b: transpose_v(b, 0))
-            vv_turn(turn, 0, lambda b: transpose_v(b, 1))
+            vv_turn(turn, 0, lambda b: transpose_v(b, 0))
+            vv_turn(turn, 1, lambda b: transpose_v(b, 1))
             unit_stage(turn - 1, transpose_p)
         b = B - 1
         u = UNITS - 1
         reciprocal(u)
         normalise(u)
-        multiply_pv(b - 1, [1])
+        multiply_pv(b - 1, [2])
         group_p(u - 1)
         quantise_p(u - 1)
         transpose_p(u)
         store_out(b - 1, [0])
-        multiply_pv(b - 1, [2, 3])
+        multiply_pv(b - 1, [3])
         group_p(u)
         quantise_p(u, parts=2)
         store_out(b - 1, [1,2,3], vector=[2])
         for i in range(CHUNKS):
             multiply_pv(b, [i])
-            store_out(b, [i], vector=[0, 2])
+            store_out(b, [i], vector=[0,2])

from contextlib import ExitStack

import concourse.mybir as mybir
from concourse.masks import make_identity

F32 = mybir.dt.float32
BF16 = mybir.dt.bfloat16
U32 = mybir.dt.uint32
U8 = mybir.dt.uint8
FP8X4 = mybir.dt.float8_e4m3fn_x4
ALU = mybir.AluOpType
AX = mybir.AxisListType
ACT = mybir.ActivationFunctionType

P = 128
PACK = 4
NH, B, S, D = 3, 8, 512, 128
AHEAD = 5
H = 512
V = 512
CHUNKS = S // P
UNITS = B * NH
FIRST = [P * i * (i + 1) // 2 for i in range(CHUNKS)]
WIDTH = P * CHUNKS * (CHUNKS + 1) // 2
P_FIRST = [0, 256, 512, 1024]
P_WIDTH = 1536
SCALE = D ** -0.5
MASKED = -1.0e30

FLOPS = 2 * (B * S * H * V + NH * B * S * S * D + NH * B * S * S * V)


def tile_interpretablemultiheadattention_pa_t_kernel(tc, qh, kh, v, Wv, bv, out):
    nc = tc.nc
    with ExitStack() as ctx:
        const = ctx.enter_context(tc.tile_pool(name="const", bufs=1))
        inputs = ctx.enter_context(tc.tile_pool(name="inputs", bufs=1))
        per_unit = ctx.enter_context(tc.tile_pool(name="per_unit", bufs=3))
        per_batch = ctx.enter_context(tc.tile_pool(name="per_batch", bufs=2))
        stores = ctx.enter_context(tc.tile_pool(name="stores", bufs=8))
        psum_low = ctx.enter_context(tc.psum_pool(name="psum_low", bufs=1))
        psum = ctx.enter_context(tc.psum_pool(name="psum", bufs=7))
        ctx.enter_context(tc.manual_schedule())

        v_sb, q_sb, k_sb = [], [], []
        w_raw = const.tile([P, PACK, V], BF16)
        bias = const.tile([P, V], BF16)
        bias_row = const.tile([P, V], BF16)
        nc.gpsimd.memset(bias_row[:], 0.0)
        ones = const.tile([P, P], BF16)
        nc.gpsimd.memset(ones[:], 1.0)

        def load_v(b):
            v_b = inputs.tile([P, CHUNKS, H], BF16, name="v%d" % b)
            nc.sync.dma_start(
                out=v_b[:].rearrange("p (u e) h -> p u e h", u=2),
                in_=v[b].rearrange("(u p e) h -> p u e h", u=2, e=2),
            )
            v_sb.append(v_b)

        def load(unit):
            b, n = divmod(unit, NH)
            q_u = inputs.tile([P, CHUNKS, D], BF16, name="q%d" % unit)
            nc.sync.dma_start(out=q_u[:], in_=qh[n, b].rearrange("(c p) d -> p c d", p=P))
            q_sb.append(q_u)
            k_u = inputs.tile([P, CHUNKS, D], BF16, name="k%d" % unit)
            nc.sync.dma_start(out=k_u[:], in_=kh[n, b].rearrange("(c p) d -> p c d", p=P))
            k_sb.append(k_u)
            if unit == NH - 1:
                load_v(0)
                nc.sync.dma_start(
                    out=w_raw[:].rearrange("q (u e) c -> q u e c", u=2),
                    in_=Wv.rearrange("(u q e) c -> q u e c", u=2, e=2),
                )
                nc.sync.dma_start(out=bias_row[0:1, :], in_=bv.unsqueeze(0))
            if n == 1 and b > 0:
                load_v(b)

        for unit in range(AHEAD - 1):
            load(unit)

        ident_bf = const.tile([P, P], BF16)
        make_identity(nc, ident_bf[:])
        mask_f32 = const.tile([P, P], F32)
        nc.gpsimd.memset(mask_f32[:], 0.0)
        nc.gpsimd.affine_select(
            out=mask_f32[:],
            in_=mask_f32[:],
            compare_op=ALU.is_ge,
            fill=MASKED,
            base=0,
            pattern=[[-1, P]],
            channel_multiplier=1,
        )
        mask_bf = const.tile([P, P], BF16)
        nc.vector.tensor_copy(out=mask_bf[:], in_=mask_f32[:])
        ident_f32 = const.tile([P, P], F32)
        make_identity(nc, ident_f32[:])
        p_bf16 = []
        for x in range(3):
            g = const.tile([P, P_WIDTH], BF16, name="p_bf%d" % x, align_bytes=64)
            nc.gpsimd.memset(g[:, 128:256], 0.0)
            nc.gpsimd.memset(g[:, P_FIRST[2] + 384 : P_FIRST[2] + 512], 0.0)
            p_bf16.append(g)
        zeros = const.tile([P, P], F32, align_bytes=64)
        nc.gpsimd.memset(zeros[:], 0.0)
        low = psum_low.tile([P, 2, 2, P], F32, name="low")

        def clear_low():
            for i in range(2):
                nc.tensor.transpose(low[:, 1, i, :], zeros[:], ident_f32[:])

        w_grouped = const.tile([P, V, PACK], BF16, align_bytes=64)
        w_codes = const.tile([P, V], U32, align_bytes=64)
        w_scales = const.tile([P, V], U8, align_bytes=64)

        live = {}

        def transpose_v(b, half):
            v_words = v_sb[b][:].rearrange("p c h -> p (c h)").bitcast(F32)
            vt = psum.tile([P, 2, 2, P], F32, name="vt", tag="bank")
            for c in range(2):
                for u in range(2):
                    first = (2 * half + c) * (H // 2) + u * P
                    nc.tensor.transpose(vt[:, c, u, :], v_words[:, first : first + P], ident_f32[:])
            live["vt", b, half] = vt

        def group_v(b, half):
            if half == 0:
                live["v_grouped", b] = per_batch.tile(
                    [P, S, PACK], BF16, name="v_grouped", align_bytes=64
                )
            words = live["v_grouped", b][:].rearrange("p r t -> p (r t)").bitcast(F32)
            nc.scalar.copy(
                out=words[:, half * S : (half + 1) * S].rearrange(
                    "p (c r u) -> p c r u", c=2, u=2
                ),
                in_=live["vt", b, half][:].rearrange("p c u r -> p c r u"),
            )

        def spread_bias():
            spread = psum.tile([P, V], F32, name="spread", tag="bank")
            nc.tensor.matmul(out=spread[:], lhsT=ones[:], rhs=bias_row[:], start=True, stop=True)
            nc.scalar.copy(out=bias[:], in_=spread[:])

        def group_w():
            nc.vector.tensor_copy(out=w_grouped[:], in_=w_raw[:].rearrange("q t c -> q c t"))

        def quantise_w():
            nc.vector.quantize_mx(
                out=w_codes[:].bitcast(FP8X4),
                scales=w_scales[:],
                in_=w_grouped[:].rearrange("q c t -> q (c t)"),
            )

        def quantise_v(b):
            v_codes = per_batch.tile([P, S], U32, name="v_codes", align_bytes=64)
            v_scales = per_batch.tile([P, S], U8, name="v_scales", align_bytes=64)
            nc.vector.quantize_mx(
                out=v_codes[:].bitcast(FP8X4),
                scales=v_scales[:],
                in_=live["v_grouped", b][:].rearrange("p r t -> p (r t)"),
            )
            live["v_codes", b] = v_codes
            live["v_scales", b] = v_scales

        def multiply_vv(b, pieces):
            for w in pieces:
                cols = slice(w * P, (w + 1) * P)
                vv_ps = psum.tile([P, PACK, P], F32, name="vv_ps", tag="bank")
                for t in range(PACK):
                    toks = slice(t * P, (t + 1) * P)
                    nc.tensor.matmul_mx(
                        out=vv_ps[:, t, :],
                        lhsT=live["v_codes", b][:, toks].bitcast(FP8X4),
                        lhsT_scale=live["v_scales", b][:, toks],
                        rhs=w_codes[:, cols].bitcast(FP8X4),
                        rhs_scale=w_scales[:, cols],
                        start=True,
                        stop=True,
                    )
                live["vv_ps", b, w] = vv_ps

        def add_bias(b, pieces):
            if 0 in pieces:
                live["vv_grouped", b] = per_batch.tile(
                    [P, V, PACK], BF16, name="vv_grouped", align_bytes=64
                )
            for w in pieces:
                cols = slice(w * P, (w + 1) * P)
                nc.vector.tensor_tensor(
                    out=live["vv_grouped", b][:, cols, :],
                    in0=live["vv_ps", b, w][:].rearrange("p t c -> p c t"),
                    in1=bias[:, cols].unsqueeze(2).to_broadcast([P, P, PACK]),
                    op=ALU.add,
                )

        def quantise_vv(b):
            vv_codes = per_batch.tile([P, V], U32, name="vv_codes", align_bytes=64)
            vv_scales = per_batch.tile([P, V], U8, name="vv_scales", align_bytes=64)
            nc.vector.quantize_mx(
                out=vv_codes[:].bitcast(FP8X4),
                scales=vv_scales[:],
                in_=live["vv_grouped", b][:].rearrange("p c t -> p (c t)"),
            )
            live["vv_codes", b] = vv_codes
            live["vv_scales", b] = vv_scales

        def transpose_qk(unit):
            qk_ps = psum.tile([P, 2, S], BF16, name="qk_ps", tag="bank")
            for x, blocks in enumerate([q_sb[unit], k_sb[unit]]):
                for c in range(CHUNKS):
                    turned = qk_ps[:, x, c * P : (c + 1) * P]
                    if x == 0:
                        nc.tensor.matmul(
                            out=turned, lhsT=blocks[:, c, :], rhs=ident_bf[:], start=True, stop=True
                        )
                    else:
                        nc.tensor.transpose(turned, blocks[:, c, :], ident_bf[:])
            live["qk_ps", unit] = qk_ps

        def copy_qk(unit):
            qk_t = per_unit.tile([P, 2, S], BF16, name="qk_t")
            nc.scalar.copy(out=qk_t[:], in_=live["qk_ps", unit][:])
            live["qk_t", unit] = qk_t

        SCORE_BANKS = [[3], [2, 0], [1]]

        def scores(unit):
            qk_t = live["qk_t", unit]
            for blocks in SCORE_BANKS:
                sc = psum.tile([P, S], F32, name="sc", tag="bank")
                first = 0
                for i in blocks:
                    keys = (i + 1) * P
                    rows = slice(i * P, (i + 1) * P)
                    nc.tensor.matmul(
                        out=sc[:, first : first + keys],
                        lhsT=qk_t[:, 0, rows],
                        rhs=qk_t[:, 1, 0:keys],
                        start=True,
                        stop=False,
                    )
                    nc.tensor.matmul(
                        out=sc[:, first + i * P : first + keys],
                        lhsT=ident_bf[:],
                        rhs=mask_bf[:],
                        start=False,
                        stop=True,
                    )
                    live["sc", unit, i] = sc[:, first : first + keys]
                    first += keys

        def row_max(unit):
            neg_max = per_unit.tile([P, CHUNKS], F32, name="neg_max")
            e = per_unit.tile([P, WIDTH], F32, name="e")
            for blocks in SCORE_BANKS:
                for i in blocks:
                    nc.vector.tensor_scalar(
                        out=e[:, FIRST[i] : FIRST[i] + (i + 1) * P],
                        in0=live["sc", unit, i],
                        scalar1=-SCALE,
                        scalar2=None,
                        op0=ALU.mult,
                        op1=ALU.min,
                        accum_out=neg_max[:, i : i + 1],
                    )
            live["neg_max", unit] = neg_max
            live["e", unit] = e

        def exponential(unit):
            row_sum = per_unit.tile([P, CHUNKS], F32, name="row_sum")
            e = live["e", unit]
            for blocks in SCORE_BANKS:
                for i in blocks:
                    cols = slice(FIRST[i], FIRST[i] + (i + 1) * P)
                    nc.scalar.activation(
                        out=e[:, cols],
                        in_=e[:, cols],
                        func=ACT.Exp,
                        bias=live["neg_max", unit][:, i : i + 1],
                        scale=-1.0,
                        accum_out=row_sum[:, i : i + 1],
                    )
            live["row_sum", unit] = row_sum

        def reciprocal(unit):
            inv_sum = per_unit.tile([P, CHUNKS], F32, name="inv_sum")
            nc.vector.reciprocal(out=inv_sum[:], in_=live["row_sum", unit][:])
            live["inv_sum", unit] = inv_sum

        P_BANKS = [[2, 3], [0, 1]]

        def normalise(unit):
            last = unit == UNITS - 1
            for blocks in P_BANKS:
                for i in blocks:
                    keys = (i + 1) * P
                    p_i = p_bf16[unit % 3][:, P_FIRST[i] : P_FIRST[i] + keys]
                    e_i = live["e", unit][:, FIRST[i] : FIRST[i] + keys]
                    inv_i = live["inv_sum", unit][:, i : i + 1]
                    if (i % 2 == 1) if last else (i < 2):
                        nc.vector.tensor_scalar_mul(out=p_i, in0=e_i, scalar1=inv_i)
                    elif last:
                        nc.scalar.activation(out=p_i, in_=e_i, func=ACT.Copy, scale=inv_i)
                    else:
                        nc.gpsimd.tensor_scalar(
                            out=p_i, in0=e_i, scalar1=inv_i, scalar2=0.0, op0=ALU.mult, op1=ALU.add
                        )

        def transpose_p(unit):
            p_words = p_bf16[unit % 3][:].bitcast(F32)
            pt = psum.tile([P, 2, 2, P], F32, name="pt", tag="bank")
            for y, i in enumerate(P_BANKS[0]):
                for u in range(2):
                    first = P_FIRST[i] // 2 + u * P
                    nc.tensor.transpose(pt[:, y, u, :], p_words[:, first : first + P], ident_f32[:])
            live["pt", unit] = pt
            for i in P_BANKS[1]:
                first = P_FIRST[i] // 2
                nc.tensor.transpose(low[:, 0, i, :], p_words[:, first : first + P], ident_f32[:])

        def group_p(unit):
            p_grouped = per_unit.tile([P, S, PACK], BF16, name="p_grouped", align_bytes=64)
            words = p_grouped[:].rearrange("p q t -> p (q t)").bitcast(F32)
            (nc.scalar.copy if unit % 3 != 1 and unit < UNITS - 1 else nc.vector.tensor_copy)(
                out=words[:, S : 2 * S].rearrange("p (i q u) -> p i q u", i=2, u=2),
                in_=live["pt", unit][:].rearrange("p i u q -> p i q u"),
            )
            nc.scalar.copy(
                out=words[:, 0:S].rearrange("p (i q u) -> p i q u", i=2, u=2),
                in_=low[:].rearrange("p u i q -> p i q u"),
            )
            live["p_grouped", unit] = p_grouped

        def quantise_p(unit, parts=1):
            p_codes = per_unit.tile([P, S], U32, name="p_codes", bufs=2 * NH, align_bytes=64)
            p_scales = per_unit.tile([P, S], U8, name="p_scales", bufs=2 * NH, align_bytes=64)
            n = S // parts
            for x in range(parts):
                rows = slice(x * n, (x + 1) * n)
                nc.vector.quantize_mx(
                    out=p_codes[:, rows].bitcast(FP8X4),
                    scales=p_scales[:, rows],
                    in_=live["p_grouped", unit][:, rows, :].rearrange("p q t -> p (q t)"),
                )
            live["p_codes", unit] = p_codes
            live["p_scales", unit] = p_scales

        def multiply_pv(b, blocks):
            for i in blocks:
                rows = slice(i * P, (i + 1) * P)
                acc = psum.tile([P, V], F32, name="acc", tag="bank")
                for n in range(NH):
                    nc.tensor.matmul_mx(
                        out=acc[:],
                        lhsT=live["p_codes", b * NH + n][:, rows].bitcast(FP8X4),
                        lhsT_scale=live["p_scales", b * NH + n][:, rows],
                        rhs=live["vv_codes", b][:].bitcast(FP8X4),
                        rhs_scale=live["vv_scales", b][:],
                        start=(n == 0),
                        stop=(n == NH - 1),
                    )
                live["acc", b, i] = acc

        def store_out(b, blocks, vector=()):
            for i in blocks:
                result = stores.tile([P, V], F32, name="result")
                if i in vector:
                    nc.vector.tensor_scalar_mul(out=result[:], in0=live["acc", b, i][:], scalar1=1.0 / NH)
                else:
                    nc.scalar.mul(out=result[:], in_=live["acc", b, i][:], mul=1.0 / NH)
                nc.sync.dma_start(out=out[b, i * P : (i + 1) * P, :], in_=result[:])

        def unit_stage(unit, stage):
            if 0 <= unit < UNITS:
                stage(unit)

        def vv_turn(turn, step, stage):
            for b in range(B):
                if turn == max(2 * b, NH * (b - 1)) + step:
                    stage(b)

        def pv_turn(turn, stage):
            b, third = divmod(turn - 5, NH)
            blocks = PV0[third] if b == 0 else [[0, 1], [2], [3]][third]
            if 0 <= b < B and blocks:
                stage(b, blocks)

        PV0 = [[], [0, 1], [2, 3]]
        for turn in range(-2, UNITS):
            unit_stage(turn + AHEAD + 1, load)
            unit_stage(turn - 1, reciprocal)
            unit_stage(turn - 1, normalise)
            pv_turn(turn - 1, store_out)
            unit_stage(turn + 1, copy_qk)
            unit_stage(turn - 2, group_p)
            vv_turn(turn, 1, lambda b: group_v(b, 0))
            vv_turn(turn, 2, lambda b: group_v(b, 1))
            unit_stage(turn, scores)
            if turn == 0:
                clear_low()
            unit_stage(turn, row_max)
            unit_stage(turn, exponential)
            if turn == 1:
                spread_bias()
                group_w()
                quantise_w()
            unit_stage(turn - 2, quantise_p)
            vv_turn(turn, 2, quantise_v)
            vv_turn(turn, 5, quantise_vv)
            pv_turn(turn, multiply_pv)
            vv_turn(turn, 3, lambda b: multiply_vv(b, [0, 1]))
            vv_turn(turn, 4, lambda b: multiply_vv(b, [2, 3]))
            vv_turn(turn, 3, lambda b: add_bias(b, [0, 1]))
            vv_turn(turn, 4, lambda b: add_bias(b, [2, 3]))
            unit_stage(turn + 2, transpose_qk)
            vv_turn(turn, 0, lambda b: transpose_v(b, 0))
            vv_turn(turn, 1, lambda b: transpose_v(b, 1))
            unit_stage(turn - 1, transpose_p)
        b = B - 1
        u = UNITS - 1
        reciprocal(u)
        normalise(u)
        multiply_pv(b - 1, [2])
        group_p(u - 1)
        quantise_p(u - 1)
        transpose_p(u)
        store_out(b - 1, [0])
        multiply_pv(b - 1, [3])
        group_p(u)
        quantise_p(u, parts=2)
        store_out(b - 1, [1,2,3], vector=[2])
        for i in range(CHUNKS):
            multiply_pv(b, [i])
            store_out(b, [i], vector=[0,2])
